import numpy as np
import ml_dtypes


def mxq(x, axis, fmt="e4m3"):
    dtype, down = {"e4m3": (ml_dtypes.float8_e4m3fn, 7), "e5m2": (ml_dtypes.float8_e5m2, 14)}[fmt]
    v = np.moveaxis(np.asarray(x, np.float32).astype(ml_dtypes.bfloat16).astype(np.float64), axis, -1)
    blocks = v.reshape(v.shape[:-1] + (-1, 32))
    amax = np.abs(blocks).max(-1, keepdims=True)
    byte = np.maximum(np.where(amax > 0, np.frexp(amax)[1] - 1 + 127, 0) - down, 1)
    scale = np.exp2(byte - 127.0)
    codes = (blocks / scale).astype(np.float32).astype(dtype).astype(np.float64)
    return np.moveaxis((codes * scale).reshape(v.shape), -1, axis)


WIDE = False


def mx_kscale(k):
    if not WIDE:
        return np.ones(k)
    levels = np.array([10, -10, 5, -5, 0])
    a = np.random.permutation(np.resize(levels, k // 512 * 4)).reshape(k // 512, 4)
    idx = np.arange(k)
    return np.exp2(a[idx // 512, idx % 128 // 32])


BF16 = ml_dtypes.bfloat16


def bf(x):
    return np.asarray(x, np.float32).astype(BF16)


def f64(x):
    return np.asarray(x).astype(np.float64)


B, C, ROWS, COLS, H, W = 16, 16, 128, 128, 16, 32
K = ROWS * COLS
N = H * W
DENSITY = 0.1


def setup_inputs():
    s = mx_kscale(K)
    image = np.random.standard_normal((B, C, K)) * s
    votes = (np.random.random_sample((K, N)) < DENSITY) * (1.0 + 0.25 * np.random.standard_normal((K, N))) / s[:, None]
    return {"image": bf(image.reshape(B, C, ROWS, COLS)), "vote_index": bf(votes.reshape(ROWS, COLS, H, W))}


def reference(image, vote_index):
    rows, cols, h, w = vote_index.shape
    b, c = image.shape[0], image.shape[1]
    V = f64(vote_index).reshape(rows * cols, h * w)
    x = np.maximum(f64(image).reshape(b * c, rows * cols), 0.0)
    ht = (mxq(x, 1, "e4m3") @ mxq(V, 0, "e4m3")) / cols
    return ht.reshape(b, c, h, w)

@@ -1,0 +1,183 @@
+from contextlib import ExitStack
+
+import concourse.mybir as mybir
+from concourse.masks import make_identity
+
+BF16 = mybir.dt.bfloat16
+F32 = mybir.dt.float32
+U32 = mybir.dt.uint32
+U8 = mybir.dt.uint8
+FP8X4 = mybir.dt.float8_e4m3fn_x4
+RELU = mybir.ActivationFunctionType.Relu
+
+P = 128
+PACK = 4
+K_PASS = P * PACK
+M = 256
+M_TILES = M // P
+K = 16384
+N = 512
+IMAGE_COLS = 128
+
+ROUND = 4
+ROUNDS = K // (K_PASS * ROUND)
+K_ROUND = K_PASS * ROUND
+PAIR = 2
+PAIRS = ROUND // PAIR
+V_PASS = PACK * N
+X_PASS = PACK * M
+RUN = 4
+AHEAD = 3
+
+FLOPS = 2 * M * K * N
+
+
+def tile_ht_k_kernel(tc, image, vote_index, out):
+    nc = tc.nc
+    x_dram = image.rearrange("b c r w -> (b c) (r w)").rearrange("(m p) k -> p m k", p=P)
+    v_dram = vote_index.rearrange("r c h w -> (r c) (h w)")
+    out_dram = out.rearrange("b c h w -> (b c) (h w)")
+
+    with ExitStack() as ctx:
+        consts = ctx.enter_context(tc.tile_pool(name="consts", bufs=1))
+        x_raw_pool = ctx.enter_context(tc.tile_pool(name="x_raw", bufs=AHEAD))
+        v_raw_pool = ctx.enter_context(tc.tile_pool(name="v_raw", bufs=PAIRS * (AHEAD + 1)))
+        grouped_pool = ctx.enter_context(tc.tile_pool(name="grouped", bufs=2))
+        v_grouped_pool = ctx.enter_context(tc.tile_pool(name="v_grouped", bufs=2 * PAIRS))
+        x_mx_pool = ctx.enter_context(tc.tile_pool(name="x_mx", bufs=2))
+        v_mx_pool = ctx.enter_context(tc.tile_pool(name="v_mx", bufs=2 * PAIRS))
+        result_pool = ctx.enter_context(tc.tile_pool(name="result", bufs=M_TILES))
+        acc_pool = ctx.enter_context(tc.psum_pool(name="acc", bufs=1))
+        xt_pool = ctx.enter_context(tc.psum_pool(name="xt", bufs=6))
+
+        ident = consts.tile([P, P], F32)
+        make_identity(nc, ident[:])
+
+        acc = [acc_pool.tile([P, N], F32, name="acc%d" % m) for m in range(M_TILES)]
+
+        x_raw_of = {}
+        v_raw_of = {}
+        xt_of = {}
+        x_grouped_of = {}
+        x_mx_of = {}
+        v_grouped_of = {}
+        v_mx_of = {}
+
+        def load(r):
+            x_raw = x_raw_pool.tile([P, M_TILES * K_ROUND], BF16)
+            nc.sync.dma_start(
+                out=x_raw[:].rearrange("p (m k) -> p m k", m=M_TILES),
+                in_=x_dram[:, :, r * K_ROUND : (r + 1) * K_ROUND],
+            )
+            x_raw_of[r] = x_raw
+            for h in range(PAIRS):
+                v_raw = v_raw_pool.tile([P, PAIR * V_PASS], BF16)
+                first_row = r * K_ROUND + h * PAIR * K_PASS
+                nc.sync.dma_start(
+                    out=v_raw[:].rearrange("p (g f) -> p g f", g=PAIR),
+                    in_=v_dram[first_row : first_row + PAIR * K_PASS, :].rearrange(
+                        "(g p j) n -> p g (j n)", p=P, j=PACK
+                    ),
+                )
+                v_raw_of[r, h] = v_raw
+
+        def transpose_x(r):
+            words = x_raw_of[r][:].bitcast(F32).rearrange(
+                "p (m g q u) -> p m g u q", m=M_TILES, g=ROUND, u=2
+            )
+            for g in range(ROUND):
+                xt = xt_pool.tile([P, 2 * M], F32)
+                for u in range(2):
+                    for m in range(M_TILES):
+                        nc.tensor.transpose(
+                            out=xt[:, u * M + m * P : u * M + (m + 1) * P],
+                            in_=words[:, m, g, u, :],
+                            identity=ident[:],
+                        )
+                xt_of[r, g] = xt
+
+        def relu_x(r):
+            x_grouped = grouped_pool.tile([P, ROUND * X_PASS], BF16, align_bytes=64)
+            for g in range(ROUND):
+                nc.scalar.activation(
+                    out=x_grouped[:, g * X_PASS : (g + 1) * X_PASS].rearrange(
+                        "p (r u e) -> p r u e", u=2, e=2
+                    ),
+                    in_=xt_of[r, g][:].bitcast(BF16).rearrange("p (u r e) -> p r u e", u=2, e=2),
+                    func=RELU,
+                )
+            x_grouped_of[r] = x_grouped
+
+        def quantise_x(r):
+            x_codes = x_mx_pool.tile([P, ROUND * M], U32, align_bytes=64)
+            x_scales = x_mx_pool.tile([P, ROUND * M], U8, align_bytes=64)
+            nc.vector.quantize_mx(
+                out=x_codes[:].bitcast(FP8X4), scales=x_scales[:], in_=x_grouped_of[r][:]
+            )
+            x_mx_of[r] = (x_codes, x_scales)
+
+        def regroup_v(r):
+            for h in range(PAIRS):
+                v_grouped = v_grouped_pool.tile([P, PAIR * V_PASS], BF16, align_bytes=64)
+                for g in range(PAIR):
+                    last_of_round = h == PAIRS - 1 and g == PAIR - 1
+                    copy = nc.scalar.copy if last_of_round else nc.vector.tensor_copy
+                    copy(
+                        out=v_grouped[:, g * V_PASS : (g + 1) * V_PASS].rearrange(
+                            "p (c i t) -> p c t i", i=RUN, t=PACK
+                        ),
+                        in_=v_raw_of[r, h][:, g * V_PASS : (g + 1) * V_PASS].rearrange(
+                            "p (t c i) -> p c t i", t=PACK, i=RUN
+                        ),
+                    )
+                v_grouped_of[r, h] = v_grouped
+
+        def quantise_v(r):
+            for h in range(PAIRS):
+                v_codes = v_mx_pool.tile([P, PAIR * N], U32, align_bytes=64)
+                v_scales = v_mx_pool.tile([P, PAIR * N], U8, align_bytes=64)
+                nc.vector.quantize_mx(
+                    out=v_codes[:].bitcast(FP8X4), scales=v_scales[:], in_=v_grouped_of[r, h][:]
+                )
+                v_mx_of[r, h] = (v_codes, v_scales)
+
+        def multiply(r):
+            x_codes, x_scales = x_mx_of[r]
+            for g in range(ROUND):
+                v_codes, v_scales = v_mx_of[r, g // PAIR]
+                n_cols = slice((g % PAIR) * N, (g % PAIR + 1) * N)
+                for m in range(M_TILES):
+                    m_cols = slice(g * M + m * P, g * M + (m + 1) * P)
+                    nc.tensor.matmul_mx(
+                        out=acc[m][:],
+                        lhsT=x_codes[:, m_cols].bitcast(FP8X4),
+                        lhsT_scale=x_scales[:, m_cols],
+                        rhs=v_codes[:, n_cols].bitcast(FP8X4),
+                        rhs_scale=v_scales[:, n_cols],
+                        start=(r == 0 and g == 0),
+                        stop=(r == ROUNDS - 1 and g == ROUND - 1),
+                    )
+
+        for r in range(AHEAD):
+            load(r)
+        transpose_x(0)
+        relu_x(0)
+        for r in range(ROUNDS):
+            if r + AHEAD < ROUNDS:
+                load(r + AHEAD)
+            if r + 1 < ROUNDS:
+                transpose_x(r + 1)
+            regroup_v(r)
+            if r + 1 < ROUNDS:
+                relu_x(r + 1)
+            quantise_x(r)
+            quantise_v(r)
+            multiply(r)
+
+        for m in range(M_TILES):
+            result = result_pool.tile([P, N], F32)
+            if m == 0:
+                nc.vector.tensor_scalar_mul(out=result[:], in0=acc[m][:], scalar1=1.0 / IMAGE_COLS)
+            else:
+                nc.scalar.mul(out=result[:], in_=acc[m][:], mul=1.0 / IMAGE_COLS)
+            nc.sync.dma_start(out=out_dram[m * P : (m + 1) * P, :], in_=result[:])

@@ -19,15 +19,14 @@ K = 16384
 N = 512
 IMAGE_COLS = 128
 
-ROUND = 4
-ROUNDS = K // (K_PASS * ROUND)
-K_ROUND = K_PASS * ROUND
 PAIR = 2
-PAIRS = ROUND // PAIR
+STEPS = K // (K_PASS * PAIR)
+X_CHUNK = 2
 V_PASS = PACK * N
 X_PASS = PACK * M
 RUN = 4
-AHEAD = 3
+SCALAR_COLS = 128
+AHEAD = 6
 
 FLOPS = 2 * M * K * N
 
@@ -39,13 +38,14 @@ def tile_ht_k_kernel(tc, image, vote_index, out):
     out_dram = out.rearrange("b c h w -> (b c) (h w)")
 
     with ExitStack() as ctx:
+        ctx.enter_context(tc.manual_schedule())
         consts = ctx.enter_context(tc.tile_pool(name="consts", bufs=1))
-        x_raw_pool = ctx.enter_context(tc.tile_pool(name="x_raw", bufs=AHEAD))
-        v_raw_pool = ctx.enter_context(tc.tile_pool(name="v_raw", bufs=PAIRS * (AHEAD + 1)))
-        grouped_pool = ctx.enter_context(tc.tile_pool(name="grouped", bufs=2))
-        v_grouped_pool = ctx.enter_context(tc.tile_pool(name="v_grouped", bufs=2 * PAIRS))
-        x_mx_pool = ctx.enter_context(tc.tile_pool(name="x_mx", bufs=2))
-        v_mx_pool = ctx.enter_context(tc.tile_pool(name="v_mx", bufs=2 * PAIRS))
+        x_raw_pool = ctx.enter_context(tc.tile_pool(name="x_raw", bufs=AHEAD // X_CHUNK + 1))
+        v_raw_pool = ctx.enter_context(tc.tile_pool(name="v_raw", bufs=PAIR * (AHEAD + 1)))
+        x_grouped_pool = ctx.enter_context(tc.tile_pool(name="x_grouped", bufs=3))
+        v_grouped_pool = ctx.enter_context(tc.tile_pool(name="v_grouped", bufs=3))
+        x_mx_pool = ctx.enter_context(tc.tile_pool(name="x_mx", bufs=3))
+        v_mx_pool = ctx.enter_context(tc.tile_pool(name="v_mx", bufs=3))
         result_pool = ctx.enter_context(tc.tile_pool(name="result", bufs=M_TILES))
         acc_pool = ctx.enter_context(tc.psum_pool(name="acc", bufs=1))
         xt_pool = ctx.enter_context(tc.psum_pool(name="xt", bufs=6))
@@ -55,97 +55,104 @@ def tile_ht_k_kernel(tc, image, vote_index, out):
 
         acc = [acc_pool.tile([P, N], F32, name="acc%d" % m) for m in range(M_TILES)]
 
-        x_raw_of = {}
+        x_words_of = {}
         v_raw_of = {}
         xt_of = {}
         x_grouped_of = {}
-        x_mx_of = {}
         v_grouped_of = {}
+        x_mx_of = {}
         v_mx_of = {}
 
-        def load(r):
-            x_raw = x_raw_pool.tile([P, M_TILES * K_ROUND], BF16)
-            nc.sync.dma_start(
-                out=x_raw[:].rearrange("p (m k) -> p m k", m=M_TILES),
-                in_=x_dram[:, :, r * K_ROUND : (r + 1) * K_ROUND],
-            )
-            x_raw_of[r] = x_raw
-            for h in range(PAIRS):
-                v_raw = v_raw_pool.tile([P, PAIR * V_PASS], BF16)
-                first_row = r * K_ROUND + h * PAIR * K_PASS
+        def load(s):
+            if s < X_CHUNK:
+                chunk_steps = 1
+            elif s % X_CHUNK == 0:
+                chunk_steps = X_CHUNK
+            else:
+                chunk_steps = 0
+            if chunk_steps > 0:
+                k_chunk = chunk_steps * PAIR * K_PASS
+                x_raw = x_raw_pool.tile([P, M_TILES * k_chunk], BF16)
+                first_k = s * PAIR * K_PASS
                 nc.sync.dma_start(
-                    out=v_raw[:].rearrange("p (g f) -> p g f", g=PAIR),
-                    in_=v_dram[first_row : first_row + PAIR * K_PASS, :].rearrange(
-                        "(g p j) n -> p g (j n)", p=P, j=PACK
+                    out=x_raw[:].rearrange("p (m k) -> p m k", m=M_TILES),
+                    in_=x_dram[:, :, first_k : first_k + k_chunk],
+                )
+                words = x_raw[:].bitcast(F32).rearrange(
+                    "p (m c g q u) -> p c m g u q", m=M_TILES, c=chunk_steps, g=PAIR, u=2
+                )
+                for c in range(chunk_steps):
+                    x_words_of[s + c] = words[:, c]
+            for g in range(PAIR * s, PAIR * (s + 1)):
+                v_raw = v_raw_pool.tile([P, V_PASS], BF16)
+                nc.sync.dma_start(
+                    out=v_raw[:],
+                    in_=v_dram[g * K_PASS : (g + 1) * K_PASS, :].rearrange(
+                        "(p j) n -> p (j n)", j=PACK
                     ),
                 )
-                v_raw_of[r, h] = v_raw
+                v_raw_of[g] = v_raw
 
-        def transpose_x(r):
-            words = x_raw_of[r][:].bitcast(F32).rearrange(
-                "p (m g q u) -> p m g u q", m=M_TILES, g=ROUND, u=2
-            )
-            for g in range(ROUND):
+        def transpose_x(s):
+            for g in range(PAIR):
                 xt = xt_pool.tile([P, 2 * M], F32)
                 for u in range(2):
                     for m in range(M_TILES):
                         nc.tensor.transpose(
                             out=xt[:, u * M + m * P : u * M + (m + 1) * P],
-                            in_=words[:, m, g, u, :],
+                            in_=x_words_of[s][:, m, g, u, :],
                             identity=ident[:],
                         )
-                xt_of[r, g] = xt
+                xt_of[PAIR * s + g] = xt
 
-        def relu_x(r):
-            x_grouped = grouped_pool.tile([P, ROUND * X_PASS], BF16, align_bytes=64)
-            for g in range(ROUND):
-                nc.scalar.activation(
-                    out=x_grouped[:, g * X_PASS : (g + 1) * X_PASS].rearrange(
-                        "p (r u e) -> p r u e", u=2, e=2
-                    ),
-                    in_=xt_of[r, g][:].bitcast(BF16).rearrange("p (u r e) -> p r u e", u=2, e=2),
-                    func=RELU,
-                )
-            x_grouped_of[r] = x_grouped
-
-        def quantise_x(r):
-            x_codes = x_mx_pool.tile([P, ROUND * M], U32, align_bytes=64)
-            x_scales = x_mx_pool.tile([P, ROUND * M], U8, align_bytes=64)
-            nc.vector.quantize_mx(
-                out=x_codes[:].bitcast(FP8X4), scales=x_scales[:], in_=x_grouped_of[r][:]
+        def relu_x(s, g):
+            if g == 0:
+                x_grouped = x_grouped_pool.tile([P, PAIR * X_PASS], BF16, align_bytes=64)
+                x_grouped_of[s] = x_grouped
+            nc.scalar.activation(
+                out=x_grouped_of[s][:, g * X_PASS : (g + 1) * X_PASS].rearrange(
+                    "p (r u e) -> p r u e", u=2, e=2
+                ),
+                in_=xt_of[PAIR * s + g][:].bitcast(BF16).rearrange("p (u r e) -> p r u e", u=2, e=2),
+                func=RELU,
             )
-            x_mx_of[r] = (x_codes, x_scales)
 
-        def regroup_v(r):
-            for h in range(PAIRS):
-                v_grouped = v_grouped_pool.tile([P, PAIR * V_PASS], BF16, align_bytes=64)
-                for g in range(PAIR):
-                    last_of_round = h == PAIRS - 1 and g == PAIR - 1
-                    copy = nc.scalar.copy if last_of_round else nc.vector.tensor_copy
-                    copy(
-                        out=v_grouped[:, g * V_PASS : (g + 1) * V_PASS].rearrange(
-                            "p (c i t) -> p c t i", i=RUN, t=PACK
-                        ),
-                        in_=v_raw_of[r, h][:, g * V_PASS : (g + 1) * V_PASS].rearrange(
-                            "p (t c i) -> p c t i", t=PACK, i=RUN
-                        ),
-                    )
-                v_grouped_of[r, h] = v_grouped
+        def regroup_v(copy, s, g, first_col, last_col):
+            grouped = v_grouped_of[s][:, g * V_PASS : (g + 1) * V_PASS].rearrange(
+                "p (n t) -> p n t", t=PACK
+            )
+            rows = v_raw_of[PAIR * s + g][:].rearrange("p (t n) -> p t n", t=PACK)
+            copy(
+                out=grouped[:, first_col:last_col, :].rearrange("p (c i) t -> p c t i", i=RUN),
+                in_=rows[:, :, first_col:last_col].rearrange("p t (c i) -> p c t i", i=RUN),
+            )
 
-        def quantise_v(r):
-            for h in range(PAIRS):
+        def quantise_x(s):
+            x_codes = x_mx_pool.tile([P, PAIR * M], U32, align_bytes=64)
+            x_scales = x_mx_pool.tile([P, PAIR * M], U8, align_bytes=64)
+            nc.vector.quantize_mx(
+                out=x_codes[:].bitcast(FP8X4), scales=x_scales[:], in_=x_grouped_of[s][:]
+            )
+            x_mx_of[s] = (x_codes, x_scales)
+
+        def quantise_v(s, first_pass, passes):
+            if first_pass == 0:
                 v_codes = v_mx_pool.tile([P, PAIR * N], U32, align_bytes=64)
                 v_scales = v_mx_pool.tile([P, PAIR * N], U8, align_bytes=64)
-                nc.vector.quantize_mx(
-                    out=v_codes[:].bitcast(FP8X4), scales=v_scales[:], in_=v_grouped_of[r, h][:]
-                )
-                v_mx_of[r, h] = (v_codes, v_scales)
+                v_mx_of[s] = (v_codes, v_scales)
+            v_codes, v_scales = v_mx_of[s]
+            cols = slice(first_pass * N, (first_pass + passes) * N)
+            nc.vector.quantize_mx(
+                out=v_codes[:, cols].bitcast(FP8X4),
+                scales=v_scales[:, cols],
+                in_=v_grouped_of[s][:, first_pass * V_PASS : (first_pass + passes) * V_PASS],
+            )
 
-        def multiply(r):
-            x_codes, x_scales = x_mx_of[r]
-            for g in range(ROUND):
-                v_codes, v_scales = v_mx_of[r, g // PAIR]
-                n_cols = slice((g % PAIR) * N, (g % PAIR + 1) * N)
+        def multiply(s):
+            x_codes, x_scales = x_mx_of[s]
+            v_codes, v_scales = v_mx_of[s]
+            for g in range(PAIR):
+                n_cols = slice(g * N, (g + 1) * N)
                 for m in range(M_TILES):
                     m_cols = slice(g * M + m * P, g * M + (m + 1) * P)
                     nc.tensor.matmul_mx(
@@ -154,25 +161,37 @@ def tile_ht_k_kernel(tc, image, vote_index, out):
                         lhsT_scale=x_scales[:, m_cols],
                         rhs=v_codes[:, n_cols].bitcast(FP8X4),
                         rhs_scale=v_scales[:, n_cols],
-                        start=(r == 0 and g == 0),
-                        stop=(r == ROUNDS - 1 and g == ROUND - 1),
+                        start=(s == 0 and g == 0),
+                        stop=(s == STEPS - 1 and g == PAIR - 1),
                     )
 
-        for r in range(AHEAD):
-            load(r)
-        transpose_x(0)
-        relu_x(0)
-        for r in range(ROUNDS):
-            if r + AHEAD < ROUNDS:
-                load(r + AHEAD)
-            if r + 1 < ROUNDS:
-                transpose_x(r + 1)
-            regroup_v(r)
-            if r + 1 < ROUNDS:
-                relu_x(r + 1)
-            quantise_x(r)
-            quantise_v(r)
-            multiply(r)
+        for s in range(AHEAD - 1):
+            load(s)
+        for s in range(-1, STEPS + 1):
+            if s + AHEAD < STEPS:
+                load(s + AHEAD)
+            if s + 1 < STEPS:
+                transpose_x(s + 1)
+            if s >= 1:
+                multiply(s - 1)
+            if 0 <= s < STEPS:
+                v_grouped = v_grouped_pool.tile([P, PAIR * V_PASS], BF16, align_bytes=64)
+                v_grouped_of[s] = v_grouped
+                for g in range(PAIR):
+                    regroup_v(nc.scalar.copy, s, g, N - SCALAR_COLS, N)
+            if s + 1 < STEPS:
+                for g in range(PAIR):
+                    relu_x(s + 1, g)
+            if 0 <= s < STEPS - 1:
+                for g in range(PAIR):
+                    regroup_v(nc.vector.tensor_copy, s, g, 0, N - SCALAR_COLS)
+                quantise_x(s)
+                quantise_v(s, 0, PAIR)
+            if s == STEPS - 1:
+                quantise_x(s)
+                for g in range(PAIR):
+                    regroup_v(nc.vector.tensor_copy, s, g, 0, N - SCALAR_COLS)
+                    quantise_v(s, g, 1)
 
         for m in range(M_TILES):
             result = result_pool.tile([P, N], F32)

@@ -25,7 +25,7 @@ X_CHUNK = 2
 V_PASS = PACK * N
 X_PASS = PACK * M
 RUN = 4
-SCALAR_COLS = 128
+SCALAR_COLS = 144
 AHEAD = 6
 
 FLOPS = 2 * M * K * N
@@ -41,9 +41,9 @@ def tile_ht_k_kernel(tc, image, vote_index, out):
         ctx.enter_context(tc.manual_schedule())
         consts = ctx.enter_context(tc.tile_pool(name="consts", bufs=1))
         x_raw_pool = ctx.enter_context(tc.tile_pool(name="x_raw", bufs=AHEAD // X_CHUNK + 1))
-        v_raw_pool = ctx.enter_context(tc.tile_pool(name="v_raw", bufs=PAIR * (AHEAD + 1)))
-        x_grouped_pool = ctx.enter_context(tc.tile_pool(name="x_grouped", bufs=3))
-        v_grouped_pool = ctx.enter_context(tc.tile_pool(name="v_grouped", bufs=3))
+        v_raw_pool = ctx.enter_context(tc.tile_pool(name="v_raw", bufs=AHEAD + 1))
+        x_grouped_pool = ctx.enter_context(tc.tile_pool(name="x_grouped", bufs=4))
+        v_grouped_pool = ctx.enter_context(tc.tile_pool(name="v_grouped", bufs=4))
         x_mx_pool = ctx.enter_context(tc.tile_pool(name="x_mx", bufs=3))
         v_mx_pool = ctx.enter_context(tc.tile_pool(name="v_mx", bufs=3))
         result_pool = ctx.enter_context(tc.tile_pool(name="result", bufs=M_TILES))
@@ -83,15 +83,16 @@ def tile_ht_k_kernel(tc, image, vote_index, out):
                 )
                 for c in range(chunk_steps):
                     x_words_of[s + c] = words[:, c]
-            for g in range(PAIR * s, PAIR * (s + 1)):
-                v_raw = v_raw_pool.tile([P, V_PASS], BF16)
+            v_raw = v_raw_pool.tile([P, PAIR * V_PASS], BF16)
+            for g in range(PAIR):
+                first_row = (PAIR * s + g) * K_PASS
                 nc.sync.dma_start(
-                    out=v_raw[:],
-                    in_=v_dram[g * K_PASS : (g + 1) * K_PASS, :].rearrange(
+                    out=v_raw[:, g * V_PASS : (g + 1) * V_PASS],
+                    in_=v_dram[first_row : first_row + K_PASS, :].rearrange(
                         "(p j) n -> p (j n)", j=PACK
                     ),
                 )
-                v_raw_of[g] = v_raw
+            v_raw_of[s] = v_raw
 
         def transpose_x(s):
             for g in range(PAIR):
@@ -121,10 +122,18 @@ def tile_ht_k_kernel(tc, image, vote_index, out):
             grouped = v_grouped_of[s][:, g * V_PASS : (g + 1) * V_PASS].rearrange(
                 "p (n t) -> p n t", t=PACK
             )
-            rows = v_raw_of[PAIR * s + g][:].rearrange("p (t n) -> p t n", t=PACK)
+            rows = v_raw_of[s][:, g * V_PASS : (g + 1) * V_PASS].rearrange("p (t n) -> p t n", t=PACK)
             copy(
                 out=grouped[:, first_col:last_col, :].rearrange("p (c i) t -> p c t i", i=RUN),
                 in_=rows[:, :, first_col:last_col].rearrange("p t (c i) -> p c t i", i=RUN),
+            )
+
+        def regroup_v_both_passes(s, first_col, last_col):
+            grouped = v_grouped_of[s][:].rearrange("p (g n t) -> p g n t", g=PAIR, t=PACK)
+            rows = v_raw_of[s][:].rearrange("p (g t n) -> p g t n", g=PAIR, t=PACK)
+            nc.vector.tensor_copy(
+                out=grouped[:, :, first_col:last_col, :].rearrange("p g (c i) t -> p g c t i", i=RUN),
+                in_=rows[:, :, :, first_col:last_col].rearrange("p g t (c i) -> p g c t i", i=RUN),
             )
 
         def quantise_x(s):
@@ -167,11 +176,12 @@ def tile_ht_k_kernel(tc, image, vote_index, out):
 
         for s in range(AHEAD - 1):
             load(s)
+        transpose_x(0)
         for s in range(-1, STEPS + 1):
             if s + AHEAD < STEPS:
                 load(s + AHEAD)
-            if s + 1 < STEPS:
-                transpose_x(s + 1)
+            if s + 2 < STEPS:
+                transpose_x(s + 2)
             if s >= 1:
                 multiply(s - 1)
             if 0 <= s < STEPS:
@@ -183,8 +193,11 @@ def tile_ht_k_kernel(tc, image, vote_index, out):
                 for g in range(PAIR):
                     relu_x(s + 1, g)
             if 0 <= s < STEPS - 1:
-                for g in range(PAIR):
-                    regroup_v(nc.vector.tensor_copy, s, g, 0, N - SCALAR_COLS)
+                if s == 0:
+                    for g in range(PAIR):
+                        regroup_v(nc.vector.tensor_copy, s, g, 0, N - SCALAR_COLS)
+                else:
+                    regroup_v_both_passes(s, 0, N - SCALAR_COLS)
                 quantise_x(s)
                 quantise_v(s, 0, PAIR)
             if s == STEPS - 1:

@@ -25,7 +25,7 @@ X_CHUNK = 2
 V_PASS = PACK * N
 X_PASS = PACK * M
 RUN = 4
-SCALAR_COLS = 144
+SCALAR_COLS = 128
 AHEAD = 6
 
 FLOPS = 2 * M * K * N
@@ -41,7 +41,7 @@ def tile_ht_k_kernel(tc, image, vote_index, out):
         ctx.enter_context(tc.manual_schedule())
         consts = ctx.enter_context(tc.tile_pool(name="consts", bufs=1))
         x_raw_pool = ctx.enter_context(tc.tile_pool(name="x_raw", bufs=AHEAD // X_CHUNK + 1))
-        v_raw_pool = ctx.enter_context(tc.tile_pool(name="v_raw", bufs=AHEAD + 1))
+        v_raw_pool = ctx.enter_context(tc.tile_pool(name="v_raw", bufs=PAIR * (AHEAD + 1)))
         x_grouped_pool = ctx.enter_context(tc.tile_pool(name="x_grouped", bufs=4))
         v_grouped_pool = ctx.enter_context(tc.tile_pool(name="v_grouped", bufs=4))
         x_mx_pool = ctx.enter_context(tc.tile_pool(name="x_mx", bufs=3))
@@ -83,16 +83,15 @@ def tile_ht_k_kernel(tc, image, vote_index, out):
                 )
                 for c in range(chunk_steps):
                     x_words_of[s + c] = words[:, c]
-            v_raw = v_raw_pool.tile([P, PAIR * V_PASS], BF16)
-            for g in range(PAIR):
-                first_row = (PAIR * s + g) * K_PASS
+            for g in range(PAIR * s, PAIR * (s + 1)):
+                v_raw = v_raw_pool.tile([P, V_PASS], BF16)
                 nc.sync.dma_start(
-                    out=v_raw[:, g * V_PASS : (g + 1) * V_PASS],
-                    in_=v_dram[first_row : first_row + K_PASS, :].rearrange(
+                    out=v_raw[:],
+                    in_=v_dram[g * K_PASS : (g + 1) * K_PASS, :].rearrange(
                         "(p j) n -> p (j n)", j=PACK
                     ),
                 )
-            v_raw_of[s] = v_raw
+                v_raw_of[g] = v_raw
 
         def transpose_x(s):
             for g in range(PAIR):
@@ -122,18 +121,10 @@ def tile_ht_k_kernel(tc, image, vote_index, out):
             grouped = v_grouped_of[s][:, g * V_PASS : (g + 1) * V_PASS].rearrange(
                 "p (n t) -> p n t", t=PACK
             )
-            rows = v_raw_of[s][:, g * V_PASS : (g + 1) * V_PASS].rearrange("p (t n) -> p t n", t=PACK)
+            rows = v_raw_of[PAIR * s + g][:].rearrange("p (t n) -> p t n", t=PACK)
             copy(
                 out=grouped[:, first_col:last_col, :].rearrange("p (c i) t -> p c t i", i=RUN),
                 in_=rows[:, :, first_col:last_col].rearrange("p t (c i) -> p c t i", i=RUN),
-            )
-
-        def regroup_v_both_passes(s, first_col, last_col):
-            grouped = v_grouped_of[s][:].rearrange("p (g n t) -> p g n t", g=PAIR, t=PACK)
-            rows = v_raw_of[s][:].rearrange("p (g t n) -> p g t n", g=PAIR, t=PACK)
-            nc.vector.tensor_copy(
-                out=grouped[:, :, first_col:last_col, :].rearrange("p g (c i) t -> p g c t i", i=RUN),
-                in_=rows[:, :, :, first_col:last_col].rearrange("p g t (c i) -> p g c t i", i=RUN),
             )
 
         def quantise_x(s):
@@ -157,22 +148,21 @@ def tile_ht_k_kernel(tc, image, vote_index, out):
                 in_=v_grouped_of[s][:, first_pass * V_PASS : (first_pass + passes) * V_PASS],
             )
 
-        def multiply(s):
+        def multiply(s, g):
             x_codes, x_scales = x_mx_of[s]
             v_codes, v_scales = v_mx_of[s]
-            for g in range(PAIR):
-                n_cols = slice(g * N, (g + 1) * N)
-                for m in range(M_TILES):
-                    m_cols = slice(g * M + m * P, g * M + (m + 1) * P)
-                    nc.tensor.matmul_mx(
-                        out=acc[m][:],
-                        lhsT=x_codes[:, m_cols].bitcast(FP8X4),
-                        lhsT_scale=x_scales[:, m_cols],
-                        rhs=v_codes[:, n_cols].bitcast(FP8X4),
-                        rhs_scale=v_scales[:, n_cols],
-                        start=(s == 0 and g == 0),
-                        stop=(s == STEPS - 1 and g == PAIR - 1),
-                    )
+            n_cols = slice(g * N, (g + 1) * N)
+            for m in range(M_TILES):
+                m_cols = slice(g * M + m * P, g * M + (m + 1) * P)
+                nc.tensor.matmul_mx(
+                    out=acc[m][:],
+                    lhsT=x_codes[:, m_cols].bitcast(FP8X4),
+                    lhsT_scale=x_scales[:, m_cols],
+                    rhs=v_codes[:, n_cols].bitcast(FP8X4),
+                    rhs_scale=v_scales[:, n_cols],
+                    start=(s == 0 and g == 0),
+                    stop=(s == STEPS - 1 and g == PAIR - 1),
+                )
 
         for s in range(AHEAD - 1):
             load(s)
@@ -180,10 +170,12 @@ def tile_ht_k_kernel(tc, image, vote_index, out):
         for s in range(-1, STEPS + 1):
             if s + AHEAD < STEPS:
                 load(s + AHEAD)
+            if s >= 1:
+                multiply(s - 1, 0)
             if s + 2 < STEPS:
                 transpose_x(s + 2)
             if s >= 1:
-                multiply(s - 1)
+                multiply(s - 1, 1)
             if 0 <= s < STEPS:
                 v_grouped = v_grouped_pool.tile([P, PAIR * V_PASS], BF16, align_bytes=64)
                 v_grouped_of[s] = v_grouped
@@ -192,19 +184,15 @@ def tile_ht_k_kernel(tc, image, vote_index, out):
             if s + 1 < STEPS:
                 for g in range(PAIR):
                     relu_x(s + 1, g)
-            if 0 <= s < STEPS - 1:
-                if s == 0:
-                    for g in range(PAIR):
-                        regroup_v(nc.vector.tensor_copy, s, g, 0, N - SCALAR_COLS)
-                else:
-                    regroup_v_both_passes(s, 0, N - SCALAR_COLS)
-                quantise_x(s)
-                quantise_v(s, 0, PAIR)
-            if s == STEPS - 1:
-                quantise_x(s)
+            if 0 <= s < STEPS:
                 for g in range(PAIR):
                     regroup_v(nc.vector.tensor_copy, s, g, 0, N - SCALAR_COLS)
-                    quantise_v(s, g, 1)
+                quantise_x(s)
+                if s < STEPS - 1:
+                    quantise_v(s, 0, PAIR)
+                else:
+                    for g in range(PAIR):
+                        quantise_v(s, g, 1)
 
         for m in range(M_TILES):
             result = result_pool.tile([P, N], F32)

from contextlib import ExitStack

import concourse.mybir as mybir
from concourse.masks import make_identity

BF16 = mybir.dt.bfloat16
F32 = mybir.dt.float32
U32 = mybir.dt.uint32
U8 = mybir.dt.uint8
FP8X4 = mybir.dt.float8_e4m3fn_x4
RELU = mybir.ActivationFunctionType.Relu

P = 128
PACK = 4
K_PASS = P * PACK
M = 256
M_TILES = M // P
K = 16384
N = 512
IMAGE_COLS = 128

PAIR = 2
STEPS = K // (K_PASS * PAIR)
X_CHUNK = 2
V_PASS = PACK * N
X_PASS = PACK * M
RUN = 4
SCALAR_COLS = 128
AHEAD = 6

FLOPS = 2 * M * K * N


def tile_ht_k_kernel(tc, image, vote_index, out):
    nc = tc.nc
    x_dram = image.rearrange("b c r w -> (b c) (r w)").rearrange("(m p) k -> p m k", p=P)
    v_dram = vote_index.rearrange("r c h w -> (r c) (h w)")
    out_dram = out.rearrange("b c h w -> (b c) (h w)")

    with ExitStack() as ctx:
        ctx.enter_context(tc.manual_schedule())
        consts = ctx.enter_context(tc.tile_pool(name="consts", bufs=1))
        x_raw_pool = ctx.enter_context(tc.tile_pool(name="x_raw", bufs=AHEAD // X_CHUNK + 1))
        v_raw_pool = ctx.enter_context(tc.tile_pool(name="v_raw", bufs=PAIR * (AHEAD + 1)))
        x_grouped_pool = ctx.enter_context(tc.tile_pool(name="x_grouped", bufs=4))
        v_grouped_pool = ctx.enter_context(tc.tile_pool(name="v_grouped", bufs=4))
        x_mx_pool = ctx.enter_context(tc.tile_pool(name="x_mx", bufs=3))
        v_mx_pool = ctx.enter_context(tc.tile_pool(name="v_mx", bufs=3))
        result_pool = ctx.enter_context(tc.tile_pool(name="result", bufs=M_TILES))
        acc_pool = ctx.enter_context(tc.psum_pool(name="acc", bufs=1))
        xt_pool = ctx.enter_context(tc.psum_pool(name="xt", bufs=6))

        ident = consts.tile([P, P], F32)
        make_identity(nc, ident[:])

        acc = [acc_pool.tile([P, N], F32, name="acc%d" % m) for m in range(M_TILES)]

        x_words_of = {}
        v_raw_of = {}
        xt_of = {}
        x_grouped_of = {}
        v_grouped_of = {}
        x_mx_of = {}
        v_mx_of = {}

        def load(s):
            if s < X_CHUNK:
                chunk_steps = 1
            elif s % X_CHUNK == 0:
                chunk_steps = X_CHUNK
            else:
                chunk_steps = 0
            if chunk_steps > 0:
                k_chunk = chunk_steps * PAIR * K_PASS
                x_raw = x_raw_pool.tile([P, M_TILES * k_chunk], BF16)
                first_k = s * PAIR * K_PASS
                nc.sync.dma_start(
                    out=x_raw[:].rearrange("p (m k) -> p m k", m=M_TILES),
                    in_=x_dram[:, :, first_k : first_k + k_chunk],
                )
                words = x_raw[:].bitcast(F32).rearrange(
                    "p (m c g q u) -> p c m g u q", m=M_TILES, c=chunk_steps, g=PAIR, u=2
                )
                for c in range(chunk_steps):
                    x_words_of[s + c] = words[:, c]
            for g in range(PAIR * s, PAIR * (s + 1)):
                v_raw = v_raw_pool.tile([P, V_PASS], BF16)
                nc.sync.dma_start(
                    out=v_raw[:],
                    in_=v_dram[g * K_PASS : (g + 1) * K_PASS, :].rearrange(
                        "(p j) n -> p (j n)", j=PACK
                    ),
                )
                v_raw_of[g] = v_raw

        def transpose_x(s):
            for g in range(PAIR):
                xt = xt_pool.tile([P, 2 * M], F32)
                for u in range(2):
                    for m in range(M_TILES):
                        nc.tensor.transpose(
                            out=xt[:, u * M + m * P : u * M + (m + 1) * P],
                            in_=x_words_of[s][:, m, g, u, :],
                            identity=ident[:],
                        )
                xt_of[PAIR * s + g] = xt

        def relu_x(s, g):
            if g == 0:
                x_grouped = x_grouped_pool.tile([P, PAIR * X_PASS], BF16, align_bytes=64)
                x_grouped_of[s] = x_grouped
            nc.scalar.activation(
                out=x_grouped_of[s][:, g * X_PASS : (g + 1) * X_PASS].rearrange(
                    "p (r u e) -> p r u e", u=2, e=2
                ),
                in_=xt_of[PAIR * s + g][:].bitcast(BF16).rearrange("p (u r e) -> p r u e", u=2, e=2),
                func=RELU,
            )

        def regroup_v(copy, s, g, first_col, last_col):
            grouped = v_grouped_of[s][:, g * V_PASS : (g + 1) * V_PASS].rearrange(
                "p (n t) -> p n t", t=PACK
            )
            rows = v_raw_of[PAIR * s + g][:].rearrange("p (t n) -> p t n", t=PACK)
            copy(
                out=grouped[:, first_col:last_col, :].rearrange("p (c i) t -> p c t i", i=RUN),
                in_=rows[:, :, first_col:last_col].rearrange("p t (c i) -> p c t i", i=RUN),
            )

        def quantise_x(s):
            x_codes = x_mx_pool.tile([P, PAIR * M], U32, align_bytes=64)
            x_scales = x_mx_pool.tile([P, PAIR * M], U8, align_bytes=64)
            nc.vector.quantize_mx(
                out=x_codes[:].bitcast(FP8X4), scales=x_scales[:], in_=x_grouped_of[s][:]
            )
            x_mx_of[s] = (x_codes, x_scales)

        def quantise_v(s, first_pass, passes):
            if first_pass == 0:
                v_codes = v_mx_pool.tile([P, PAIR * N], U32, align_bytes=64)
                v_scales = v_mx_pool.tile([P, PAIR * N], U8, align_bytes=64)
                v_mx_of[s] = (v_codes, v_scales)
            v_codes, v_scales = v_mx_of[s]
            cols = slice(first_pass * N, (first_pass + passes) * N)
            nc.vector.quantize_mx(
                out=v_codes[:, cols].bitcast(FP8X4),
                scales=v_scales[:, cols],
                in_=v_grouped_of[s][:, first_pass * V_PASS : (first_pass + passes) * V_PASS],
            )

        def multiply(s, g):
            x_codes, x_scales = x_mx_of[s]
            v_codes, v_scales = v_mx_of[s]
            n_cols = slice(g * N, (g + 1) * N)
            for m in range(M_TILES):
                m_cols = slice(g * M + m * P, g * M + (m + 1) * P)
                nc.tensor.matmul_mx(
                    out=acc[m][:],
                    lhsT=x_codes[:, m_cols].bitcast(FP8X4),
                    lhsT_scale=x_scales[:, m_cols],
                    rhs=v_codes[:, n_cols].bitcast(FP8X4),
                    rhs_scale=v_scales[:, n_cols],
                    start=(s == 0 and g == 0),
                    stop=(s == STEPS - 1 and g == PAIR - 1),
                )

        for s in range(AHEAD - 1):
            load(s)
        transpose_x(0)
        for s in range(-1, STEPS + 1):
            if s + AHEAD < STEPS:
                load(s + AHEAD)
            if s >= 1:
                multiply(s - 1, 0)
            if s + 2 < STEPS:
                transpose_x(s + 2)
            if s >= 1:
                multiply(s - 1, 1)
            if 0 <= s < STEPS:
                v_grouped = v_grouped_pool.tile([P, PAIR * V_PASS], BF16, align_bytes=64)
                v_grouped_of[s] = v_grouped
                for g in range(PAIR):
                    regroup_v(nc.scalar.copy, s, g, N - SCALAR_COLS, N)
            if s + 1 < STEPS:
                for g in range(PAIR):
                    relu_x(s + 1, g)
            if 0 <= s < STEPS:
                for g in range(PAIR):
                    regroup_v(nc.vector.tensor_copy, s, g, 0, N - SCALAR_COLS)
                quantise_x(s)
                if s < STEPS - 1:
                    quantise_v(s, 0, PAIR)
                else:
                    for g in range(PAIR):
                        quantise_v(s, g, 1)

        for m in range(M_TILES):
            result = result_pool.tile([P, N], F32)
            if m == 0:
                nc.vector.tensor_scalar_mul(out=result[:], in0=acc[m][:], scalar1=1.0 / IMAGE_COLS)
            else:
                nc.scalar.mul(out=result[:], in_=acc[m][:], mul=1.0 / IMAGE_COLS)
            nc.sync.dma_start(out=out_dram[m * P : (m + 1) * P, :], in_=result[:])
